import numpy as np
import ml_dtypes

BF16 = ml_dtypes.bfloat16


def bf(x):
    return np.asarray(x, np.float32).astype(BF16)


def f32(x):
    return np.asarray(x, np.float32)


def f64(x):
    return np.asarray(x).astype(np.float64)


def striped(idx):
    return np.tile(idx.reshape(-1, 16).T, (8, 1))


C, S, L, B, M, T, N, H, K = 256, 2048, 32, 32, 7, 256, 8192, 1024, 8


def position_encoding():
    chan = np.arange(1, C + 1, dtype=np.float64)[:, None]
    word = np.arange(1, L + 1, dtype=np.float64)[None, :]
    return 1.0 + 4.0 * (chan - (C + 1) / 2.0) * (word - (L + 1) / 2.0) / (C * L)


def setup_inputs():
    return {"table": f32(0.1 * np.random.standard_normal((C, S))), "pe": f32(position_encoding()), "qmask": f32(np.random.uniform(0.5, 1.5, (1, B * L))), "offs": striped(np.concatenate([np.random.permutation(S)[:H] for _ in range(K)]))}


def reference(table, pe, qmask, offs):
    idx = offs[:16].T.reshape(-1)
    weight = np.tile(f64(pe), (1, T))
    weight[:, :B * L] = weight[:, :B * L] * f64(qmask)
    return (f64(table)[:, idx] * weight).reshape(C, T, L).sum(axis=2)

@@ -1,0 +1,63 @@
+import concourse.mybir as mybir
+
+F32 = mybir.dt.float32
+U16 = mybir.dt.uint16
+MULT = mybir.AluOpType.mult
+X = mybir.AxisListType.X
+
+P = 128
+BLOCKS = 2
+VOCAB = 2048
+WORDS = 32
+LIST = 8192
+PIECE = 1024
+PIECES = LIST // PIECE
+SENTENCES = PIECE // WORDS
+
+
+def tile_n2n_kernel(tc, table, pe, qmask, offs, out):
+    nc = tc.nc
+    with (
+        tc.tile_pool(name="held", bufs=1) as held,
+        tc.tile_pool(name="ring", bufs=2) as ring,
+    ):
+        offsets = held.tile([P, LIST // 16], U16, name="offsets")
+        nc.sync.dma_start(offsets[:], offs)
+
+        mask = held.tile([P, PIECE], F32, name="mask")
+        nc.sync.dma_start(mask[:], qmask.rearrange("one j -> (one j)").partition_broadcast(P))
+
+        tables, encodings = [], []
+        for b in range(BLOCKS):
+            channels = slice(b * P, (b + 1) * P)
+            encoding = held.tile([P, WORDS], F32, name=f"encoding{b}")
+            nc.sync.dma_start(encoding[:], pe[channels, :])
+            encodings.append(encoding)
+            window = held.tile([P, VOCAB], F32, name=f"table{b}")
+            nc.scalar.dma_start(window[:], table[channels, :])
+            tables.append(window)
+
+        for b in range(BLOCKS):
+            weight = held.tile([P, PIECE], F32, name=f"weight{b}")
+            nc.vector.tensor_copy(
+                weight[:].rearrange("p (t l) -> p t l", l=WORDS),
+                encodings[b][:].unsqueeze(1).to_broadcast([P, SENTENCES, WORDS]),
+            )
+            query_weight = held.tile([P, PIECE], F32, name=f"query_weight{b}")
+            nc.vector.tensor_tensor(query_weight[:], weight[:], mask[:], MULT)
+
+            encoded = held.tile([P, PIECES * SENTENCES], F32, name=f"encoded{b}")
+            for k in range(PIECES):
+                weighted = ring.tile([P, PIECE], F32, name="weighted")
+                nc.vector.tensor_tensor(
+                    weighted[:],
+                    tables[b][:].indirect(offsets[:, k * (PIECE // 16) : (k + 1) * (PIECE // 16)]),
+                    query_weight[:] if k == 0 else weight[:],
+                    MULT,
+                )
+                nc.vector.reduce_sum(
+                    encoded[:, k * SENTENCES : (k + 1) * SENTENCES],
+                    weighted[:].rearrange("p (t l) -> p t l", l=WORDS),
+                    axis=X,
+                )
+            nc.sync.dma_start(out[b * P : (b + 1) * P, :], encoded[:])

@@ -1,4 +1,5 @@
 import concourse.mybir as mybir
+from concourse.masks import make_identity
 
 F32 = mybir.dt.float32
 U16 = mybir.dt.uint16
@@ -11,21 +12,22 @@ VOCAB = 2048
 WORDS = 32
 LIST = 8192
 PIECE = 1024
-PIECES = LIST // PIECE
-SENTENCES = PIECE // WORDS
+GROUP = 2 * PIECE
+GROUPS = LIST // GROUP
+SENTENCES = GROUP // WORDS
+
+FLOPS = 2 * BLOCKS * P * LIST
 
 
 def tile_n2n_kernel(tc, table, pe, qmask, offs, out):
     nc = tc.nc
     with (
         tc.tile_pool(name="held", bufs=1) as held,
-        tc.tile_pool(name="ring", bufs=2) as ring,
+        tc.tile_pool(name="ring", bufs=3) as ring,
+        tc.psum_pool(name="psum", bufs=BLOCKS) as psum,
     ):
         offsets = held.tile([P, LIST // 16], U16, name="offsets")
         nc.sync.dma_start(offsets[:], offs)
-
-        mask = held.tile([P, PIECE], F32, name="mask")
-        nc.sync.dma_start(mask[:], qmask.rearrange("one j -> (one j)").partition_broadcast(P))
 
         tables, encodings = [], []
         for b in range(BLOCKS):
@@ -37,27 +39,48 @@ def tile_n2n_kernel(tc, table, pe, qmask, offs, out):
             nc.scalar.dma_start(window[:], table[channels, :])
             tables.append(window)
 
+        mask = held.tile([P, PIECE], F32, name="mask")
+        nc.sync.dma_start(mask[:], qmask.rearrange("one j -> (one j)").partition_broadcast(P))
+
+        identity = held.tile([P, P], F32, name="identity")
+        make_identity(nc, identity[:])
+
         for b in range(BLOCKS):
             weight = held.tile([P, PIECE], F32, name=f"weight{b}")
             nc.vector.tensor_copy(
                 weight[:].rearrange("p (t l) -> p t l", l=WORDS),
-                encodings[b][:].unsqueeze(1).to_broadcast([P, SENTENCES, WORDS]),
+                encodings[b][:].unsqueeze(1).to_broadcast([P, PIECE // WORDS, WORDS]),
             )
             query_weight = held.tile([P, PIECE], F32, name=f"query_weight{b}")
             nc.vector.tensor_tensor(query_weight[:], weight[:], mask[:], MULT)
 
-            encoded = held.tile([P, PIECES * SENTENCES], F32, name=f"encoded{b}")
-            for k in range(PIECES):
-                weighted = ring.tile([P, PIECE], F32, name="weighted")
-                nc.vector.tensor_tensor(
-                    weighted[:],
-                    tables[b][:].indirect(offsets[:, k * (PIECE // 16) : (k + 1) * (PIECE // 16)]),
-                    query_weight[:] if k == 0 else weight[:],
-                    MULT,
-                )
-                nc.vector.reduce_sum(
-                    encoded[:, k * SENTENCES : (k + 1) * SENTENCES],
-                    weighted[:].rearrange("p (t l) -> p t l", l=WORDS),
-                    axis=X,
-                )
+            sums = psum.tile([P, GROUPS * SENTENCES], F32, name="sums")
+            encoded = held.tile([P, GROUPS * SENTENCES], F32, name=f"encoded{b}")
+            summed_in_psum = 0
+            for g in range(GROUPS):
+                weighted = ring.tile([P, GROUP], F32, name="weighted")
+                for k in range(g * GROUP // PIECE, (g + 1) * GROUP // PIECE):
+                    nc.vector.tensor_tensor(
+                        weighted[:, k * PIECE - g * GROUP : (k + 1) * PIECE - g * GROUP],
+                        tables[b][:].indirect(offsets[:, k * (PIECE // 16) : (k + 1) * (PIECE // 16)]),
+                        query_weight[:] if k == 0 else weight[:],
+                        MULT,
+                    )
+
+                words = weighted[:].rearrange("p (t l) -> p t l", l=WORDS)
+                sentences = slice(g * SENTENCES, (g + 1) * SENTENCES)
+                if b == BLOCKS - 1 and g == GROUPS - 1:
+                    nc.vector.reduce_sum(encoded[:, sentences], words, axis=X)
+                else:
+                    for l in range(WORDS):
+                        nc.tensor.matmul(
+                            sums[:, sentences],
+                            identity[:],
+                            words[:, :, l],
+                            start=(l == 0),
+                            stop=(l == WORDS - 1),
+                        )
+                    summed_in_psum += SENTENCES
+
+            nc.scalar.copy(encoded[:, :summed_in_psum], sums[:, :summed_in_psum])
             nc.sync.dma_start(out[b * P : (b + 1) * P, :], encoded[:])

@@ -12,11 +12,16 @@ VOCAB = 2048
 WORDS = 32
 LIST = 8192
 PIECE = 1024
-GROUP = 2 * PIECE
-GROUPS = LIST // GROUP
-SENTENCES = GROUP // WORDS
+PIECES = LIST // PIECE
+SENTENCES = PIECE // WORDS
+GROUPS = 2
+VECTOR_PIECES = 2
 
 FLOPS = 2 * BLOCKS * P * LIST
+
+
+def by_sentence(tile):
+    return tile[:].rearrange("p (t l) -> p t l", l=WORDS)
 
 
 def tile_n2n_kernel(tc, table, pe, qmask, offs, out):
@@ -24,63 +29,86 @@ def tile_n2n_kernel(tc, table, pe, qmask, offs, out):
     with (
         tc.tile_pool(name="held", bufs=1) as held,
         tc.tile_pool(name="ring", bufs=3) as ring,
-        tc.psum_pool(name="psum", bufs=BLOCKS) as psum,
+        tc.psum_pool(name="psum", bufs=2) as psum,
     ):
+        encodings = [held.tile([P, WORDS], F32, name=f"encoding{b}") for b in range(BLOCKS)]
+        for b in range(BLOCKS):
+            nc.sync.dma_start(encodings[b][:], pe[b * P : (b + 1) * P, :])
+
         offsets = held.tile([P, LIST // 16], U16, name="offsets")
         nc.sync.dma_start(offsets[:], offs)
 
-        tables, encodings = [], []
-        for b in range(BLOCKS):
-            channels = slice(b * P, (b + 1) * P)
-            encoding = held.tile([P, WORDS], F32, name=f"encoding{b}")
-            nc.sync.dma_start(encoding[:], pe[channels, :])
-            encodings.append(encoding)
-            window = held.tile([P, VOCAB], F32, name=f"table{b}")
-            nc.scalar.dma_start(window[:], table[channels, :])
-            tables.append(window)
-
+        tables = [held.tile([P, VOCAB], F32, name=f"table{b}") for b in range(BLOCKS)]
         mask = held.tile([P, PIECE], F32, name="mask")
-        nc.sync.dma_start(mask[:], qmask.rearrange("one j -> (one j)").partition_broadcast(P))
+        nc.scalar.dma_start(tables[0][:], table[0:P, :])
+        nc.scalar.dma_start(mask[:], qmask.rearrange("one j -> (one j)").partition_broadcast(P))
+        nc.scalar.dma_start(tables[1][:], table[P : 2 * P, :])
 
         identity = held.tile([P, P], F32, name="identity")
         make_identity(nc, identity[:])
 
+        weights = [held.tile([P, PIECE], F32, name=f"weight{b}") for b in range(BLOCKS)]
         for b in range(BLOCKS):
-            weight = held.tile([P, PIECE], F32, name=f"weight{b}")
-            nc.vector.tensor_copy(
-                weight[:].rearrange("p (t l) -> p t l", l=WORDS),
-                encodings[b][:].unsqueeze(1).to_broadcast([P, PIECE // WORDS, WORDS]),
+            nc.scalar.copy(
+                by_sentence(weights[b]),
+                encodings[b][:].unsqueeze(1).to_broadcast([P, SENTENCES, WORDS]),
             )
-            query_weight = held.tile([P, PIECE], F32, name=f"query_weight{b}")
-            nc.vector.tensor_tensor(query_weight[:], weight[:], mask[:], MULT)
 
-            sums = psum.tile([P, GROUPS * SENTENCES], F32, name="sums")
-            encoded = held.tile([P, GROUPS * SENTENCES], F32, name=f"encoded{b}")
-            summed_in_psum = 0
+        query_weights = [held.tile([P, PIECE], F32, name=f"query_weight{b}") for b in range(BLOCKS)]
+        for b in range(BLOCKS):
+            for l in range(WORDS):
+                nc.scalar.mul(
+                    by_sentence(query_weights[b])[:, :, l],
+                    by_sentence(mask)[:, :, l],
+                    encodings[b][:, l : l + 1],
+                )
+
+        def look_up(b, first, count):
+            weighted = ring.tile([P, count * PIECE], F32, name="weighted")
+            for k in reversed(range(first, first + count)):
+                nc.vector.tensor_tensor(
+                    weighted[:, (k - first) * PIECE : (k - first + 1) * PIECE],
+                    tables[b][:].indirect(offsets[:, k * (PIECE // 16) : (k + 1) * (PIECE // 16)]),
+                    query_weights[b][:] if k == 0 else weights[b][:],
+                    MULT,
+                )
+            return by_sentence(weighted)
+
+        def store(b, first, count, encoded):
+            nc.sync.dma_start(
+                out[b * P : (b + 1) * P, first * SENTENCES : (first + count) * SENTENCES], encoded
+            )
+
+        for b in range(BLOCKS):
+            vector_pieces = VECTOR_PIECES if b == BLOCKS - 1 else 0
+            count = (PIECES - vector_pieces) // GROUPS
+            n = count * SENTENCES
+
             for g in range(GROUPS):
-                weighted = ring.tile([P, GROUP], F32, name="weighted")
-                for k in range(g * GROUP // PIECE, (g + 1) * GROUP // PIECE):
-                    nc.vector.tensor_tensor(
-                        weighted[:, k * PIECE - g * GROUP : (k + 1) * PIECE - g * GROUP],
-                        tables[b][:].indirect(offsets[:, k * (PIECE // 16) : (k + 1) * (PIECE // 16)]),
-                        query_weight[:] if k == 0 else weight[:],
-                        MULT,
+                first = PIECES - (g + 1) * count
+                words = look_up(b, first, count)
+
+                sums = psum.tile([P, P], F32, name="sums")
+                for l in range(WORDS):
+                    nc.tensor.matmul(
+                        sums[:n, :],
+                        words[:, :, l],
+                        identity[:],
+                        start=(l == 0),
+                        stop=(l == WORDS - 1),
+                        is_transpose=True,
                     )
 
-                words = weighted[:].rearrange("p (t l) -> p t l", l=WORDS)
-                sentences = slice(g * SENTENCES, (g + 1) * SENTENCES)
-                if b == BLOCKS - 1 and g == GROUPS - 1:
-                    nc.vector.reduce_sum(encoded[:, sentences], words, axis=X)
-                else:
-                    for l in range(WORDS):
-                        nc.tensor.matmul(
-                            sums[:, sentences],
-                            identity[:],
-                            words[:, :, l],
-                            start=(l == 0),
-                            stop=(l == WORDS - 1),
-                        )
-                    summed_in_psum += SENTENCES
+                sentence_major = ring.tile([P, P], F32, name="sentence_major")
+                nc.scalar.copy(sentence_major[:n, :], sums[:n, :])
+                turned = psum.tile([P, P], F32, name="turned")
+                nc.tensor.transpose(turned[:, :n], sentence_major[:n, :], identity[:n, :n])
+                encoded = ring.tile([P, P], F32, name="encoded")
+                nc.scalar.copy(encoded[:, :n], turned[:, :n])
+                store(b, first, count, encoded[:, :n])
 
-            nc.scalar.copy(encoded[:, :summed_in_psum], sums[:, :summed_in_psum])
-            nc.sync.dma_start(out[b * P : (b + 1) * P, :], encoded[:])
+            if vector_pieces > 0:
+                words = look_up(b, 0, vector_pieces)
+                reduced = ring.tile([P, vector_pieces * SENTENCES], F32, name="reduced")
+                nc.vector.reduce_sum(reduced[:], words, axis=X)
+                store(b, 0, vector_pieces, reduced[:])

@@ -31,9 +31,8 @@ def tile_n2n_kernel(tc, table, pe, qmask, offs, out):
         tc.tile_pool(name="ring", bufs=3) as ring,
         tc.psum_pool(name="psum", bufs=2) as psum,
     ):
-        encodings = [held.tile([P, WORDS], F32, name=f"encoding{b}") for b in range(BLOCKS)]
-        for b in range(BLOCKS):
-            nc.sync.dma_start(encodings[b][:], pe[b * P : (b + 1) * P, :])
+        encoding = held.tile([P, BLOCKS, WORDS], F32, name="encoding")
+        nc.sync.dma_start(encoding[:], pe.rearrange("(b p) l -> p b l", p=P))
 
         offsets = held.tile([P, LIST // 16], U16, name="offsets")
         nc.sync.dma_start(offsets[:], offs)
@@ -49,9 +48,9 @@ def tile_n2n_kernel(tc, table, pe, qmask, offs, out):
 
         weights = [held.tile([P, PIECE], F32, name=f"weight{b}") for b in range(BLOCKS)]
         for b in range(BLOCKS):
-            nc.scalar.copy(
+            nc.vector.tensor_copy(
                 by_sentence(weights[b]),
-                encodings[b][:].unsqueeze(1).to_broadcast([P, SENTENCES, WORDS]),
+                encoding[:, b, :].unsqueeze(1).to_broadcast([P, SENTENCES, WORDS]),
             )
 
         query_weights = [held.tile([P, PIECE], F32, name=f"query_weight{b}") for b in range(BLOCKS)]
@@ -60,7 +59,7 @@ def tile_n2n_kernel(tc, table, pe, qmask, offs, out):
                 nc.scalar.mul(
                     by_sentence(query_weights[b])[:, :, l],
                     by_sentence(mask)[:, :, l],
-                    encodings[b][:, l : l + 1],
+                    encoding[:, b, l : l + 1],
                 )
 
         def look_up(b, first, count):

@@ -14,6 +14,7 @@ LIST = 8192
 PIECE = 1024
 PIECES = LIST // PIECE
 SENTENCES = PIECE // WORDS
+RUN = VOCAB // PIECE
 GROUPS = 2
 VECTOR_PIECES = 2
 
@@ -46,29 +47,32 @@ def tile_n2n_kernel(tc, table, pe, qmask, offs, out):
         identity = held.tile([P, P], F32, name="identity")
         make_identity(nc, identity[:])
 
-        weights = [held.tile([P, PIECE], F32, name=f"weight{b}") for b in range(BLOCKS)]
+        weights = [held.tile([P, RUN * PIECE], F32, name=f"weight{b}") for b in range(BLOCKS)]
         for b in range(BLOCKS):
             nc.vector.tensor_copy(
                 by_sentence(weights[b]),
-                encoding[:, b, :].unsqueeze(1).to_broadcast([P, SENTENCES, WORDS]),
+                encoding[:, b, :].unsqueeze(1).to_broadcast([P, RUN * SENTENCES, WORDS]),
             )
 
-        query_weights = [held.tile([P, PIECE], F32, name=f"query_weight{b}") for b in range(BLOCKS)]
+        query_weights = [held.tile([P, RUN * PIECE], F32, name=f"query_weight{b}") for b in range(BLOCKS)]
         for b in range(BLOCKS):
             for l in range(WORDS):
                 nc.scalar.mul(
-                    by_sentence(query_weights[b])[:, :, l],
+                    by_sentence(query_weights[b])[:, :SENTENCES, l],
                     by_sentence(mask)[:, :, l],
                     encoding[:, b, l : l + 1],
                 )
+            nc.scalar.copy(query_weights[b][:, PIECE:], weights[b][:, PIECE:])
 
         def look_up(b, first, count):
             weighted = ring.tile([P, count * PIECE], F32, name="weighted")
-            for k in reversed(range(first, first + count)):
+            for k in reversed(range(first, first + count, RUN)):
+                run = min(RUN, first + count - k)
+                weight = query_weights[b] if k == 0 else weights[b]
                 nc.vector.tensor_tensor(
-                    weighted[:, (k - first) * PIECE : (k - first + 1) * PIECE],
-                    tables[b][:].indirect(offsets[:, k * (PIECE // 16) : (k + 1) * (PIECE // 16)]),
-                    query_weights[b][:] if k == 0 else weights[b][:],
+                    weighted[:, (k - first) * PIECE : (k - first + run) * PIECE],
+                    tables[b][:].indirect(offsets[:, k * (PIECE // 16) : (k + run) * (PIECE // 16)]),
+                    weight[:, : run * PIECE],
                     MULT,
                 )
             return by_sentence(weighted)

@@ -11,18 +11,28 @@ BLOCKS = 2
 VOCAB = 2048
 WORDS = 32
 LIST = 8192
-PIECE = 1024
-PIECES = LIST // PIECE
-SENTENCES = PIECE // WORDS
-RUN = VOCAB // PIECE
-GROUPS = 2
-VECTOR_PIECES = 2
+QUERY_WORDS = 1024
+RUN = VOCAB
+GROUP = P * WORDS
+SMALLEST = 512
 
 FLOPS = 2 * BLOCKS * P * LIST
 
 
 def by_sentence(tile):
     return tile[:].rearrange("p (t l) -> p t l", l=WORDS)
+
+
+def groups_of(b):
+    groups = []
+    left = LIST
+    while left > 0:
+        count = GROUP
+        if b == BLOCKS - 1:
+            count = min(GROUP, max(SMALLEST, left // 2))
+        groups.append((left - count, count))
+        left -= count
+    return groups
 
 
 def tile_n2n_kernel(tc, table, pe, qmask, offs, out):
@@ -39,79 +49,83 @@ def tile_n2n_kernel(tc, table, pe, qmask, offs, out):
         nc.sync.dma_start(offsets[:], offs)
 
         tables = [held.tile([P, VOCAB], F32, name=f"table{b}") for b in range(BLOCKS)]
-        mask = held.tile([P, PIECE], F32, name="mask")
+        mask = held.tile([P, QUERY_WORDS], F32, name="mask")
         nc.scalar.dma_start(tables[0][:], table[0:P, :])
         nc.scalar.dma_start(mask[:], qmask.rearrange("one j -> (one j)").partition_broadcast(P))
         nc.scalar.dma_start(tables[1][:], table[P : 2 * P, :])
 
         identity = held.tile([P, P], F32, name="identity")
         make_identity(nc, identity[:])
+        joins = {1: identity}
+        for parts in sorted(set(GROUP // count for b in range(BLOCKS) for first, count in groups_of(b))):
+            if parts > 1:
+                joins[parts] = held.tile([P, P // parts], F32, name=f"join{parts}")
+                nc.vector.reduce_sum(
+                    joins[parts][:], identity[:].rearrange("p (t h) -> p t h", h=parts), axis=X
+                )
 
-        weights = [held.tile([P, RUN * PIECE], F32, name=f"weight{b}") for b in range(BLOCKS)]
+        weights = [held.tile([P, RUN], F32, name=f"weight{b}") for b in range(BLOCKS)]
         for b in range(BLOCKS):
             nc.vector.tensor_copy(
                 by_sentence(weights[b]),
-                encoding[:, b, :].unsqueeze(1).to_broadcast([P, RUN * SENTENCES, WORDS]),
+                encoding[:, b, :].unsqueeze(1).to_broadcast([P, RUN // WORDS, WORDS]),
             )
 
-        query_weights = [held.tile([P, RUN * PIECE], F32, name=f"query_weight{b}") for b in range(BLOCKS)]
+        query_weights = [held.tile([P, RUN], F32, name=f"query_weight{b}") for b in range(BLOCKS)]
         for b in range(BLOCKS):
             for l in range(WORDS):
                 nc.scalar.mul(
-                    by_sentence(query_weights[b])[:, :SENTENCES, l],
+                    by_sentence(query_weights[b])[:, : QUERY_WORDS // WORDS, l],
                     by_sentence(mask)[:, :, l],
                     encoding[:, b, l : l + 1],
                 )
-            nc.scalar.copy(query_weights[b][:, PIECE:], weights[b][:, PIECE:])
+            nc.scalar.copy(query_weights[b][:, QUERY_WORDS:], weights[b][:, QUERY_WORDS:])
 
         def look_up(b, first, count):
-            weighted = ring.tile([P, count * PIECE], F32, name="weighted")
-            for k in reversed(range(first, first + count, RUN)):
-                run = min(RUN, first + count - k)
-                weight = query_weights[b] if k == 0 else weights[b]
+            weighted = ring.tile([P, count], F32, name="weighted")
+            for start in reversed(range(first, first + count, RUN)):
+                run = min(RUN, first + count - start)
+                weight = query_weights[b] if start < RUN else weights[b]
                 nc.vector.tensor_tensor(
-                    weighted[:, (k - first) * PIECE : (k - first + run) * PIECE],
-                    tables[b][:].indirect(offsets[:, k * (PIECE // 16) : (k + run) * (PIECE // 16)]),
-                    weight[:, : run * PIECE],
+                    weighted[:, start - first : start - first + run],
+                    tables[b][:].indirect(offsets[:, start // 16 : (start + run) // 16]),
+                    weight[:, start % RUN : start % RUN + run],
                     MULT,
                 )
-            return by_sentence(weighted)
+            return weighted
 
-        def store(b, first, count, encoded):
-            nc.sync.dma_start(
-                out[b * P : (b + 1) * P, first * SENTENCES : (first + count) * SENTENCES], encoded
-            )
+        def sum_on_tensor(weighted, count):
+            length = count // P
+            parts = WORDS // length
+
+            by_part = weighted[:].rearrange("p (s r) -> p s r", r=length)
+            part_sums = psum.tile([P, P], F32, name="part_sums")
+            for r in range(length):
+                nc.tensor.matmul(
+                    part_sums[:],
+                    by_part[:, :, r],
+                    identity[:],
+                    start=(r == 0),
+                    stop=(r == length - 1),
+                    is_transpose=True,
+                )
+            part_major = ring.tile([P, P], F32, name="part_major")
+            nc.scalar.copy(part_major[:], part_sums[:])
+
+            sums = psum.tile([P, count // WORDS], F32, name="sums")
+            nc.tensor.matmul(sums[:], part_major[:], joins[parts][:], start=True, stop=True)
+            encoded = ring.tile([P, count // WORDS], F32, name="encoded")
+            nc.scalar.copy(encoded[:], sums[:])
+            return encoded
 
         for b in range(BLOCKS):
-            vector_pieces = VECTOR_PIECES if b == BLOCKS - 1 else 0
-            count = (PIECES - vector_pieces) // GROUPS
-            n = count * SENTENCES
-
-            for g in range(GROUPS):
-                first = PIECES - (g + 1) * count
-                words = look_up(b, first, count)
-
-                sums = psum.tile([P, P], F32, name="sums")
-                for l in range(WORDS):
-                    nc.tensor.matmul(
-                        sums[:n, :],
-                        words[:, :, l],
-                        identity[:],
-                        start=(l == 0),
-                        stop=(l == WORDS - 1),
-                        is_transpose=True,
-                    )
-
-                sentence_major = ring.tile([P, P], F32, name="sentence_major")
-                nc.scalar.copy(sentence_major[:n, :], sums[:n, :])
-                turned = psum.tile([P, P], F32, name="turned")
-                nc.tensor.transpose(turned[:, :n], sentence_major[:n, :], identity[:n, :n])
-                encoded = ring.tile([P, P], F32, name="encoded")
-                nc.scalar.copy(encoded[:, :n], turned[:, :n])
-                store(b, first, count, encoded[:, :n])
-
-            if vector_pieces > 0:
-                words = look_up(b, 0, vector_pieces)
-                reduced = ring.tile([P, vector_pieces * SENTENCES], F32, name="reduced")
-                nc.vector.reduce_sum(reduced[:], words, axis=X)
-                store(b, 0, vector_pieces, reduced[:])
+            for first, count in groups_of(b):
+                weighted = look_up(b, first, count)
+                if b == BLOCKS - 1 and first == 0:
+                    encoded = ring.tile([P, count // WORDS], F32, name="reduced")
+                    nc.vector.reduce_sum(encoded[:], by_sentence(weighted), axis=X)
+                else:
+                    encoded = sum_on_tensor(weighted, count)
+                nc.sync.dma_start(
+                    out[b * P : (b + 1) * P, first // WORDS : (first + count) // WORDS], encoded[:]
+                )

@@ -14,7 +14,7 @@ LIST = 8192
 QUERY_WORDS = 1024
 RUN = VOCAB
 GROUP = P * WORDS
-SMALLEST = 512
+SMALLEST = 1024
 
 FLOPS = 2 * BLOCKS * P * LIST
 

@@ -4,6 +4,7 @@ from concourse.masks import make_identity
 F32 = mybir.dt.float32
 U16 = mybir.dt.uint16
 MULT = mybir.AluOpType.mult
+ADD = mybir.AluOpType.add
 X = mybir.AxisListType.X
 
 P = 128
@@ -57,22 +58,21 @@ def tile_n2n_kernel(tc, table, pe, qmask, offs, out):
         identity = held.tile([P, P], F32, name="identity")
         make_identity(nc, identity[:])
         joins = {1: identity}
-        for parts in sorted(set(GROUP // count for b in range(BLOCKS) for first, count in groups_of(b))):
-            if parts > 1:
-                joins[parts] = held.tile([P, P // parts], F32, name=f"join{parts}")
-                nc.vector.reduce_sum(
-                    joins[parts][:], identity[:].rearrange("p (t h) -> p t h", h=parts), axis=X
-                )
+        parts = 2
+        while parts <= GROUP // SMALLEST:
+            pairs = joins[parts // 2][:].rearrange("p (t two) -> p t two", two=2)
+            joins[parts] = held.tile([P, P // parts], F32, name=f"join{parts}")
+            nc.gpsimd.tensor_tensor(joins[parts][:], pairs[:, :, 0], pairs[:, :, 1], ADD)
+            parts *= 2
 
         weights = [held.tile([P, RUN], F32, name=f"weight{b}") for b in range(BLOCKS)]
-        for b in range(BLOCKS):
-            nc.vector.tensor_copy(
-                by_sentence(weights[b]),
-                encoding[:, b, :].unsqueeze(1).to_broadcast([P, RUN // WORDS, WORDS]),
-            )
-
         query_weights = [held.tile([P, RUN], F32, name=f"query_weight{b}") for b in range(BLOCKS)]
         for b in range(BLOCKS):
+            for_each_sentence = encoding[:, b, :].unsqueeze(1).to_broadcast([P, RUN // WORDS, WORDS])
+            if b == 0:
+                nc.vector.tensor_copy(by_sentence(weights[b]), for_each_sentence)
+            else:
+                nc.scalar.copy(by_sentence(weights[b]), for_each_sentence)
             for l in range(WORDS):
                 nc.scalar.mul(
                     by_sentence(query_weights[b])[:, : QUERY_WORDS // WORDS, l],

@@ -15,7 +15,7 @@ LIST = 8192
 QUERY_WORDS = 1024
 RUN = VOCAB
 GROUP = P * WORDS
-SMALLEST = 1024
+SMALLEST = 512
 
 FLOPS = 2 * BLOCKS * P * LIST
 
@@ -30,7 +30,7 @@ def groups_of(b):
     while left > 0:
         count = GROUP
         if b == BLOCKS - 1:
-            count = min(GROUP, max(SMALLEST, left // 2))
+            count = min(RUN, max(SMALLEST, left // 2))
         groups.append((left - count, count))
         left -= count
     return groups
@@ -94,10 +94,8 @@ def tile_n2n_kernel(tc, table, pe, qmask, offs, out):
                 )
             return weighted
 
-        def sum_on_tensor(weighted, count):
+        def sum_parts(weighted, count):
             length = count // P
-            parts = WORDS // length
-
             by_part = weighted[:].rearrange("p (s r) -> p s r", r=length)
             part_sums = psum.tile([P, P], F32, name="part_sums")
             for r in range(length):
@@ -111,21 +109,32 @@ def tile_n2n_kernel(tc, table, pe, qmask, offs, out):
                 )
             part_major = ring.tile([P, P], F32, name="part_major")
             nc.scalar.copy(part_major[:], part_sums[:])
+            return part_major
 
+        def store(encoded, b, first, count):
+            nc.sync.dma_start(
+                out[b * P : (b + 1) * P, first // WORDS : (first + count) // WORDS], encoded[:]
+            )
+
+        def join_parts(part_major, b, first, count):
+            parts = GROUP // count
             sums = psum.tile([P, count // WORDS], F32, name="sums")
             nc.tensor.matmul(sums[:], part_major[:], joins[parts][:], start=True, stop=True)
             encoded = ring.tile([P, count // WORDS], F32, name="encoded")
             nc.scalar.copy(encoded[:], sums[:])
-            return encoded
+            store(encoded, b, first, count)
 
+        unjoined = None
         for b in range(BLOCKS):
             for first, count in groups_of(b):
                 weighted = look_up(b, first, count)
                 if b == BLOCKS - 1 and first == 0:
+                    join_parts(*unjoined)
                     encoded = ring.tile([P, count // WORDS], F32, name="reduced")
                     nc.vector.reduce_sum(encoded[:], by_sentence(weighted), axis=X)
+                    store(encoded, b, first, count)
                 else:
-                    encoded = sum_on_tensor(weighted, count)
-                nc.sync.dma_start(
-                    out[b * P : (b + 1) * P, first // WORDS : (first + count) // WORDS], encoded[:]
-                )
+                    part_major = sum_parts(weighted, count)
+                    if unjoined is not None:
+                        join_parts(*unjoined)
+                    unjoined = (part_major, b, first, count)

@@ -14,6 +14,7 @@ WORDS = 32
 LIST = 8192
 QUERY_WORDS = 1024
 RUN = VOCAB
+BANK = 512
 GROUP = P * WORDS
 SMALLEST = 512
 
@@ -42,6 +43,7 @@ def tile_n2n_kernel(tc, table, pe, qmask, offs, out):
         tc.tile_pool(name="held", bufs=1) as held,
         tc.tile_pool(name="ring", bufs=3) as ring,
         tc.psum_pool(name="psum", bufs=2) as psum,
+        tc.psum_pool(name="psum_once", bufs=1) as psum_once,
     ):
         encoding = held.tile([P, BLOCKS, WORDS], F32, name="encoding")
         nc.sync.dma_start(encoding[:], pe.rearrange("(b p) l -> p b l", p=P))
@@ -50,10 +52,10 @@ def tile_n2n_kernel(tc, table, pe, qmask, offs, out):
         nc.sync.dma_start(offsets[:], offs)
 
         tables = [held.tile([P, VOCAB], F32, name=f"table{b}") for b in range(BLOCKS)]
-        mask = held.tile([P, QUERY_WORDS], F32, name="mask")
+        mask_by_word = held.tile([P, QUERY_WORDS // P], F32, name="mask_by_word")
         nc.scalar.dma_start(tables[0][:], table[0:P, :])
-        nc.scalar.dma_start(mask[:], qmask.rearrange("one j -> (one j)").partition_broadcast(P))
         nc.scalar.dma_start(tables[1][:], table[P : 2 * P, :])
+        nc.scalar.dma_start(mask_by_word[:], qmask.rearrange("one (a p) -> p (one a)", p=P))
 
         identity = held.tile([P, P], F32, name="identity")
         make_identity(nc, identity[:])
@@ -66,19 +68,41 @@ def tile_n2n_kernel(tc, table, pe, qmask, offs, out):
             parts *= 2
 
         weights = [held.tile([P, RUN], F32, name=f"weight{b}") for b in range(BLOCKS)]
-        query_weights = [held.tile([P, RUN], F32, name=f"query_weight{b}") for b in range(BLOCKS)]
         for b in range(BLOCKS):
             for_each_sentence = encoding[:, b, :].unsqueeze(1).to_broadcast([P, RUN // WORDS, WORDS])
             if b == 0:
                 nc.vector.tensor_copy(by_sentence(weights[b]), for_each_sentence)
             else:
                 nc.scalar.copy(by_sentence(weights[b]), for_each_sentence)
-            for l in range(WORDS):
-                nc.scalar.mul(
-                    by_sentence(query_weights[b])[:, : QUERY_WORDS // WORDS, l],
-                    by_sentence(mask)[:, :, l],
-                    encoding[:, b, l : l + 1],
-                )
+
+        pe_by_word = psum_once.tile([P, BLOCKS * P], F32, name="pe_by_word")
+        for b in range(BLOCKS):
+            nc.tensor.matmul(
+                pe_by_word[:, b * P : (b + 1) * P],
+                weights[b][:, :P],
+                identity[:],
+                start=True,
+                stop=True,
+                is_transpose=True,
+            )
+        weight_by_word = held.tile([P, QUERY_WORDS // P, BLOCKS * P], F32, name="weight_by_word")
+        for a in range(QUERY_WORDS // P):
+            nc.scalar.mul(weight_by_word[:, a, :], pe_by_word[:], mask_by_word[:, a : a + 1])
+
+        query_weights = [held.tile([P, RUN], F32, name=f"query_weight{b}") for b in range(BLOCKS)]
+        for b in range(BLOCKS):
+            for first in range(0, QUERY_WORDS, BANK):
+                turned = psum.tile([P, BANK], F32, name="turned")
+                for j in range(0, BANK, P):
+                    nc.tensor.matmul(
+                        turned[:, j : j + P],
+                        weight_by_word[:, (first + j) // P, b * P : (b + 1) * P],
+                        identity[:],
+                        start=True,
+                        stop=True,
+                        is_transpose=True,
+                    )
+                nc.scalar.copy(query_weights[b][:, first : first + BANK], turned[:])
             nc.scalar.copy(query_weights[b][:, QUERY_WORDS:], weights[b][:, QUERY_WORDS:])
 
         def look_up(b, first, count):

@@ -15,7 +15,6 @@ LIST = 8192
 QUERY_WORDS = 1024
 RUN = VOCAB
 BANK = 512
-GROUP = P * WORDS
 SMALLEST = 512
 
 FLOPS = 2 * BLOCKS * P * LIST
@@ -29,7 +28,7 @@ def groups_of(b):
     groups = []
     left = LIST
     while left > 0:
-        count = GROUP
+        count = RUN
         if b == BLOCKS - 1:
             count = min(RUN, max(SMALLEST, left // 2))
         groups.append((left - count, count))
@@ -41,7 +40,7 @@ def tile_n2n_kernel(tc, table, pe, qmask, offs, out):
     nc = tc.nc
     with (
         tc.tile_pool(name="held", bufs=1) as held,
-        tc.tile_pool(name="ring", bufs=3) as ring,
+        tc.tile_pool(name="ring", bufs=4) as ring,
         tc.psum_pool(name="psum", bufs=2) as psum,
         tc.psum_pool(name="psum_once", bufs=1) as psum_once,
     ):
@@ -54,14 +53,14 @@ def tile_n2n_kernel(tc, table, pe, qmask, offs, out):
         tables = [held.tile([P, VOCAB], F32, name=f"table{b}") for b in range(BLOCKS)]
         mask_by_word = held.tile([P, QUERY_WORDS // P], F32, name="mask_by_word")
         nc.scalar.dma_start(tables[0][:], table[0:P, :])
-        nc.scalar.dma_start(tables[1][:], table[P : 2 * P, :])
         nc.scalar.dma_start(mask_by_word[:], qmask.rearrange("one (a p) -> p (one a)", p=P))
+        nc.scalar.dma_start(tables[1][:], table[P : 2 * P, :])
 
         identity = held.tile([P, P], F32, name="identity")
         make_identity(nc, identity[:])
         joins = {1: identity}
         parts = 2
-        while parts <= GROUP // SMALLEST:
+        while parts <= P * WORDS // SMALLEST:
             pairs = joins[parts // 2][:].rearrange("p (t two) -> p t two", two=2)
             joins[parts] = held.tile([P, P // parts], F32, name=f"join{parts}")
             nc.gpsimd.tensor_tensor(joins[parts][:], pairs[:, :, 0], pairs[:, :, 1], ADD)
@@ -75,11 +74,16 @@ def tile_n2n_kernel(tc, table, pe, qmask, offs, out):
             else:
                 nc.scalar.copy(by_sentence(weights[b]), for_each_sentence)
 
+        some_weights = held.tile([P, BLOCKS, P], F32, name="some_weights")
+        nc.vector.tensor_copy(
+            some_weights[:].rearrange("p b (t l) -> p b t l", l=WORDS),
+            encoding[:].unsqueeze(2).to_broadcast([P, BLOCKS, P // WORDS, WORDS]),
+        )
         pe_by_word = psum_once.tile([P, BLOCKS * P], F32, name="pe_by_word")
         for b in range(BLOCKS):
             nc.tensor.matmul(
                 pe_by_word[:, b * P : (b + 1) * P],
-                weights[b][:, :P],
+                some_weights[:, b, :],
                 identity[:],
                 start=True,
                 stop=True,
@@ -92,7 +96,7 @@ def tile_n2n_kernel(tc, table, pe, qmask, offs, out):
         query_weights = [held.tile([P, RUN], F32, name=f"query_weight{b}") for b in range(BLOCKS)]
         for b in range(BLOCKS):
             for first in range(0, QUERY_WORDS, BANK):
-                turned = psum.tile([P, BANK], F32, name="turned")
+                turned = psum.tile([P, BANK], F32, name="turned", tag="part_sums")
                 for j in range(0, BANK, P):
                     nc.tensor.matmul(
                         turned[:, j : j + P],
@@ -107,15 +111,13 @@ def tile_n2n_kernel(tc, table, pe, qmask, offs, out):
 
         def look_up(b, first, count):
             weighted = ring.tile([P, count], F32, name="weighted")
-            for start in reversed(range(first, first + count, RUN)):
-                run = min(RUN, first + count - start)
-                weight = query_weights[b] if start < RUN else weights[b]
-                nc.vector.tensor_tensor(
-                    weighted[:, start - first : start - first + run],
-                    tables[b][:].indirect(offsets[:, start // 16 : (start + run) // 16]),
-                    weight[:, start % RUN : start % RUN + run],
-                    MULT,
-                )
+            weight = query_weights[b] if first < RUN else weights[b]
+            nc.vector.tensor_tensor(
+                weighted[:],
+                tables[b][:].indirect(offsets[:, first // 16 : (first + count) // 16]),
+                weight[:, first % RUN : first % RUN + count],
+                MULT,
+            )
             return weighted
 
         def sum_parts(weighted, count):
@@ -141,7 +143,7 @@ def tile_n2n_kernel(tc, table, pe, qmask, offs, out):
             )
 
         def join_parts(part_major, b, first, count):
-            parts = GROUP // count
+            parts = P * WORDS // count
             sums = psum.tile([P, count // WORDS], F32, name="sums")
             nc.tensor.matmul(sums[:], part_major[:], joins[parts][:], start=True, stop=True)
             encoded = ring.tile([P, count // WORDS], F32, name="encoded")

@@ -15,7 +15,7 @@ LIST = 8192
 QUERY_WORDS = 1024
 RUN = VOCAB
 BANK = 512
-SMALLEST = 512
+VECTOR_SUMS = 768
 
 FLOPS = 2 * BLOCKS * P * LIST
 
@@ -29,8 +29,12 @@ def groups_of(b):
     left = LIST
     while left > 0:
         count = RUN
-        if b == BLOCKS - 1:
-            count = min(RUN, max(SMALLEST, left // 2))
+        if b == BLOCKS - 1 and left == VECTOR_SUMS:
+            count = VECTOR_SUMS
+        elif b == BLOCKS - 1 and left <= RUN:
+            count = P
+            while 2 * count <= left - VECTOR_SUMS:
+                count *= 2
         groups.append((left - count, count))
         left -= count
     return groups
@@ -60,7 +64,7 @@ def tile_n2n_kernel(tc, table, pe, qmask, offs, out):
         make_identity(nc, identity[:])
         joins = {1: identity}
         parts = 2
-        while parts <= P * WORDS // SMALLEST:
+        while parts <= P * WORDS // min(count for first, count in groups_of(BLOCKS - 1)):
             pairs = joins[parts // 2][:].rearrange("p (t two) -> p t two", two=2)
             joins[parts] = held.tile([P, P // parts], F32, name=f"join{parts}")
             nc.gpsimd.tensor_tensor(joins[parts][:], pairs[:, :, 0], pairs[:, :, 1], ADD)
@@ -137,18 +141,24 @@ def tile_n2n_kernel(tc, table, pe, qmask, offs, out):
             nc.scalar.copy(part_major[:], part_sums[:])
             return part_major
 
-        def store(encoded, b, first, count):
+        encoded = [held.tile([P, LIST // WORDS], F32, name=f"encoded{b}") for b in range(BLOCKS)]
+
+        def sentences_of(b, first, count):
+            return encoded[b][:, first // WORDS : (first + count) // WORDS]
+
+        def store_run(b, first):
             nc.sync.dma_start(
-                out[b * P : (b + 1) * P, first // WORDS : (first + count) // WORDS], encoded[:]
+                out[b * P : (b + 1) * P, first // WORDS : (first + RUN) // WORDS],
+                sentences_of(b, first, RUN),
             )
 
         def join_parts(part_major, b, first, count):
             parts = P * WORDS // count
             sums = psum.tile([P, count // WORDS], F32, name="sums")
             nc.tensor.matmul(sums[:], part_major[:], joins[parts][:], start=True, stop=True)
-            encoded = ring.tile([P, count // WORDS], F32, name="encoded")
-            nc.scalar.copy(encoded[:], sums[:])
-            store(encoded, b, first, count)
+            nc.scalar.copy(sentences_of(b, first, count), sums[:])
+            if count == RUN:
+                store_run(b, first)
 
         unjoined = None
         for b in range(BLOCKS):
@@ -156,9 +166,8 @@ def tile_n2n_kernel(tc, table, pe, qmask, offs, out):
                 weighted = look_up(b, first, count)
                 if b == BLOCKS - 1 and first == 0:
                     join_parts(*unjoined)
-                    encoded = ring.tile([P, count // WORDS], F32, name="reduced")
-                    nc.vector.reduce_sum(encoded[:], by_sentence(weighted), axis=X)
-                    store(encoded, b, first, count)
+                    nc.vector.reduce_sum(sentences_of(b, first, count), by_sentence(weighted), axis=X)
+                    store_run(b, first)
                 else:
                     part_major = sum_parts(weighted, count)
                     if unjoined is not None:

@@ -4,7 +4,6 @@ from concourse.masks import make_identity
 F32 = mybir.dt.float32
 U16 = mybir.dt.uint16
 MULT = mybir.AluOpType.mult
-ADD = mybir.AluOpType.add
 X = mybir.AxisListType.X
 
 P = 128
@@ -66,8 +65,11 @@ def tile_n2n_kernel(tc, table, pe, qmask, offs, out):
         parts = 2
         while parts <= P * WORDS // min(count for first, count in groups_of(BLOCKS - 1)):
             pairs = joins[parts // 2][:].rearrange("p (t two) -> p t two", two=2)
+            added = psum.tile([P, P // parts], F32, name="added", tag="sums")
+            nc.tensor.matmul(added[:], identity[:], pairs[:, :, 0], start=True, stop=False)
+            nc.tensor.matmul(added[:], identity[:], pairs[:, :, 1], start=False, stop=True)
             joins[parts] = held.tile([P, P // parts], F32, name=f"join{parts}")
-            nc.gpsimd.tensor_tensor(joins[parts][:], pairs[:, :, 0], pairs[:, :, 1], ADD)
+            nc.scalar.copy(joins[parts][:], added[:])
             parts *= 2
 
         weights = [held.tile([P, RUN], F32, name=f"weight{b}") for b in range(BLOCKS)]

import concourse.mybir as mybir
from concourse.masks import make_identity

F32 = mybir.dt.float32
U16 = mybir.dt.uint16
MULT = mybir.AluOpType.mult
X = mybir.AxisListType.X

P = 128
BLOCKS = 2
VOCAB = 2048
WORDS = 32
LIST = 8192
QUERY_WORDS = 1024
RUN = VOCAB
BANK = 512
VECTOR_SUMS = 768

FLOPS = 2 * BLOCKS * P * LIST


def by_sentence(tile):
    return tile[:].rearrange("p (t l) -> p t l", l=WORDS)


def groups_of(b):
    groups = []
    left = LIST
    while left > 0:
        count = RUN
        if b == BLOCKS - 1 and left == VECTOR_SUMS:
            count = VECTOR_SUMS
        elif b == BLOCKS - 1 and left <= RUN:
            count = P
            while 2 * count <= left - VECTOR_SUMS:
                count *= 2
        groups.append((left - count, count))
        left -= count
    return groups


def tile_n2n_kernel(tc, table, pe, qmask, offs, out):
    nc = tc.nc
    with (
        tc.tile_pool(name="held", bufs=1) as held,
        tc.tile_pool(name="ring", bufs=4) as ring,
        tc.psum_pool(name="psum", bufs=2) as psum,
        tc.psum_pool(name="psum_once", bufs=1) as psum_once,
    ):
        encoding = held.tile([P, BLOCKS, WORDS], F32, name="encoding")
        nc.sync.dma_start(encoding[:], pe.rearrange("(b p) l -> p b l", p=P))

        offsets = held.tile([P, LIST // 16], U16, name="offsets")
        nc.sync.dma_start(offsets[:], offs)

        tables = [held.tile([P, VOCAB], F32, name=f"table{b}") for b in range(BLOCKS)]
        mask_by_word = held.tile([P, QUERY_WORDS // P], F32, name="mask_by_word")
        nc.scalar.dma_start(tables[0][:], table[0:P, :])
        nc.scalar.dma_start(mask_by_word[:], qmask.rearrange("one (a p) -> p (one a)", p=P))
        nc.scalar.dma_start(tables[1][:], table[P : 2 * P, :])

        identity = held.tile([P, P], F32, name="identity")
        make_identity(nc, identity[:])
        joins = {1: identity}
        parts = 2
        while parts <= P * WORDS // min(count for first, count in groups_of(BLOCKS - 1)):
            pairs = joins[parts // 2][:].rearrange("p (t two) -> p t two", two=2)
            added = psum.tile([P, P // parts], F32, name="added", tag="sums")
            nc.tensor.matmul(added[:], identity[:], pairs[:, :, 0], start=True, stop=False)
            nc.tensor.matmul(added[:], identity[:], pairs[:, :, 1], start=False, stop=True)
            joins[parts] = held.tile([P, P // parts], F32, name=f"join{parts}")
            nc.scalar.copy(joins[parts][:], added[:])
            parts *= 2

        weights = [held.tile([P, RUN], F32, name=f"weight{b}") for b in range(BLOCKS)]
        for b in range(BLOCKS):
            for_each_sentence = encoding[:, b, :].unsqueeze(1).to_broadcast([P, RUN // WORDS, WORDS])
            if b == 0:
                nc.vector.tensor_copy(by_sentence(weights[b]), for_each_sentence)
            else:
                nc.scalar.copy(by_sentence(weights[b]), for_each_sentence)

        some_weights = held.tile([P, BLOCKS, P], F32, name="some_weights")
        nc.vector.tensor_copy(
            some_weights[:].rearrange("p b (t l) -> p b t l", l=WORDS),
            encoding[:].unsqueeze(2).to_broadcast([P, BLOCKS, P // WORDS, WORDS]),
        )
        pe_by_word = psum_once.tile([P, BLOCKS * P], F32, name="pe_by_word")
        for b in range(BLOCKS):
            nc.tensor.matmul(
                pe_by_word[:, b * P : (b + 1) * P],
                some_weights[:, b, :],
                identity[:],
                start=True,
                stop=True,
                is_transpose=True,
            )
        weight_by_word = held.tile([P, QUERY_WORDS // P, BLOCKS * P], F32, name="weight_by_word")
        for a in range(QUERY_WORDS // P):
            nc.scalar.mul(weight_by_word[:, a, :], pe_by_word[:], mask_by_word[:, a : a + 1])

        query_weights = [held.tile([P, RUN], F32, name=f"query_weight{b}") for b in range(BLOCKS)]
        for b in range(BLOCKS):
            for first in range(0, QUERY_WORDS, BANK):
                turned = psum.tile([P, BANK], F32, name="turned", tag="part_sums")
                for j in range(0, BANK, P):
                    nc.tensor.matmul(
                        turned[:, j : j + P],
                        weight_by_word[:, (first + j) // P, b * P : (b + 1) * P],
                        identity[:],
                        start=True,
                        stop=True,
                        is_transpose=True,
                    )
                nc.scalar.copy(query_weights[b][:, first : first + BANK], turned[:])
            nc.scalar.copy(query_weights[b][:, QUERY_WORDS:], weights[b][:, QUERY_WORDS:])

        def look_up(b, first, count):
            weighted = ring.tile([P, count], F32, name="weighted")
            weight = query_weights[b] if first < RUN else weights[b]
            nc.vector.tensor_tensor(
                weighted[:],
                tables[b][:].indirect(offsets[:, first // 16 : (first + count) // 16]),
                weight[:, first % RUN : first % RUN + count],
                MULT,
            )
            return weighted

        def sum_parts(weighted, count):
            length = count // P
            by_part = weighted[:].rearrange("p (s r) -> p s r", r=length)
            part_sums = psum.tile([P, P], F32, name="part_sums")
            for r in range(length):
                nc.tensor.matmul(
                    part_sums[:],
                    by_part[:, :, r],
                    identity[:],
                    start=(r == 0),
                    stop=(r == length - 1),
                    is_transpose=True,
                )
            part_major = ring.tile([P, P], F32, name="part_major")
            nc.scalar.copy(part_major[:], part_sums[:])
            return part_major

        encoded = [held.tile([P, LIST // WORDS], F32, name=f"encoded{b}") for b in range(BLOCKS)]

        def sentences_of(b, first, count):
            return encoded[b][:, first // WORDS : (first + count) // WORDS]

        def store_run(b, first):
            nc.sync.dma_start(
                out[b * P : (b + 1) * P, first // WORDS : (first + RUN) // WORDS],
                sentences_of(b, first, RUN),
            )

        def join_parts(part_major, b, first, count):
            parts = P * WORDS // count
            sums = psum.tile([P, count // WORDS], F32, name="sums")
            nc.tensor.matmul(sums[:], part_major[:], joins[parts][:], start=True, stop=True)
            nc.scalar.copy(sentences_of(b, first, count), sums[:])
            if count == RUN:
                store_run(b, first)

        unjoined = None
        for b in range(BLOCKS):
            for first, count in groups_of(b):
                weighted = look_up(b, first, count)
                if b == BLOCKS - 1 and first == 0:
                    join_parts(*unjoined)
                    nc.vector.reduce_sum(sentences_of(b, first, count), by_sentence(weighted), axis=X)
                    store_run(b, first)
                else:
                    part_major = sum_parts(weighted, count)
                    if unjoined is not None:
                        join_parts(*unjoined)
                    unjoined = (part_major, b, first, count)
